import numpy as np
import ml_dtypes


def mxq(x, axis, fmt="e4m3"):
    dtype, down = {"e4m3": (ml_dtypes.float8_e4m3fn, 7), "e5m2": (ml_dtypes.float8_e5m2, 14)}[fmt]
    v = np.moveaxis(np.asarray(x, np.float32).astype(ml_dtypes.bfloat16).astype(np.float64), axis, -1)
    blocks = v.reshape(v.shape[:-1] + (-1, 32))
    amax = np.abs(blocks).max(-1, keepdims=True)
    byte = np.maximum(np.where(amax > 0, np.frexp(amax)[1] - 1 + 127, 0) - down, 1)
    scale = np.exp2(byte - 127.0)
    codes = (blocks / scale).astype(np.float32).astype(dtype).astype(np.float64)
    return np.moveaxis((codes * scale).reshape(v.shape), -1, axis)


WIDE = False


def mx_kscale(k):
    if not WIDE:
        return np.ones(k)
    levels = np.array([10, -10, 5, -5, 0])
    a = np.random.permutation(np.resize(levels, k // 512 * 4)).reshape(k // 512, 4)
    idx = np.arange(k)
    return np.exp2(a[idx // 512, idx % 128 // 32])


BF16 = ml_dtypes.bfloat16


def bf(x):
    return np.asarray(x, np.float32).astype(BF16)


def f64(x):
    return np.asarray(x).astype(np.float64)


B, IN, HID, OUT, LAYERS, NG = 1024, 512, 1024, 512, 2, 4
GW = NG * HID


def sigmoid(v):
    return 1.0 / (1.0 + np.exp(-v))


def setup_inputs():
    s = mx_kscale(IN)
    return {
        "regime_vector": bf(np.random.standard_normal((B, IN)) * s),
        "W_ih0": bf(np.random.standard_normal((GW, IN)) / np.sqrt(IN) / s),
        "hh_gates": bf(np.random.standard_normal(GW) * 0.5),
        "b_ih0": bf(np.random.standard_normal(GW) * 0.3),
        "b_hh0": bf(np.random.standard_normal(GW) * 0.3),
        "c_init": bf(np.random.standard_normal(HID)),
    }


def reference(regime_vector, W_ih0, hh_gates, b_ih0, b_hh0, c_init):
    gates = (mxq(f64(regime_vector), 1, "e4m3") @ mxq(f64(W_ih0).T, 0, "e4m3")) + f64(hh_gates) + (f64(b_ih0) + f64(b_hh0))
    i, f, g, o = np.split(gates, NG, axis=-1)
    i, f, o = sigmoid(i), sigmoid(f), sigmoid(o)
    g = np.tanh(g)
    c_new = f * f64(c_init) + i * g
    return o * np.tanh(c_new)

@@ -1,0 +1,256 @@
+from contextlib import ExitStack
+
+import concourse.mybir as mybir
+from concourse.masks import make_identity
+
+F32 = mybir.dt.float32
+BF16 = mybir.dt.bfloat16
+U32 = mybir.dt.uint32
+U8 = mybir.dt.uint8
+FP8X4 = mybir.dt.float8_e4m3fn_x4
+ACT = mybir.ActivationFunctionType
+ALU = mybir.AluOpType
+
+P = 128
+BATCH, K, HID, GATES = 1024, 512, 1024, 4
+PACK = 4
+BANK = 512
+PIECE = 2 * P
+X_PIECES = BATCH // PIECE
+W_PIECES = GATES * HID // PIECE
+HID_BLOCKS = HID // P
+HALVES = BATCH // BANK
+UNITS = HID_BLOCKS * HALVES
+GATE_I, GATE_F, GATE_G, GATE_O = 0, 1, 2, 3
+VECTOR_ROWS = GATES * HID // P
+
+FLOPS = 2 * BATCH * GATES * HID * K
+
+
+def tile_rdecommunicationlstm_pa_kernel(
+    tc, regime_vector, W_ih0, hh_gates, b_ih0, b_hh0, c_init, out
+):
+    nc = tc.nc
+    with ExitStack() as ctx:
+        const = ctx.enter_context(tc.tile_pool(name="const", bufs=1))
+        raw_pool = ctx.enter_context(tc.tile_pool(name="raw", bufs=X_PIECES + W_PIECES))
+        grouped_pool = ctx.enter_context(tc.tile_pool(name="grouped", bufs=4))
+        w_mx_pool = ctx.enter_context(tc.tile_pool(name="w_mx", bufs=W_PIECES))
+        cell_pool = ctx.enter_context(tc.tile_pool(name="cell", bufs=3))
+        psum = ctx.enter_context(tc.psum_pool(name="psum", bufs=1))
+        ctx.enter_context(tc.manual_schedule())
+
+        vector_rows = const.tile([P, P], BF16)
+        nc.vector.memset(vector_rows[:], 0.0)
+        for slot, vec in enumerate((hh_gates, b_ih0, b_hh0)):
+            nc.scalar.dma_start(
+                out=vector_rows[slot * VECTOR_ROWS : (slot + 1) * VECTOR_ROWS, :],
+                in_=vec.rearrange("(r c) -> r c", c=P),
+            )
+        nc.scalar.dma_start(
+            out=vector_rows[3 * VECTOR_ROWS : 3 * VECTOR_ROWS + HID_BLOCKS, :],
+            in_=c_init.rearrange("(r c) -> r c", c=P),
+        )
+
+        x_rows = regime_vector.rearrange("(c a p) k -> c p a k", a=2, p=P)
+        w_rows = W_ih0.rearrange("(h e j p) k -> j e p h k", h=2, e=2, p=P)
+
+        def load(rows):
+            raw = raw_pool.tile([P, 2 * K], BF16, tag="raw")
+            nc.sync.dma_start(out=raw[:].rearrange("p (a k) -> p a k", a=2), in_=rows)
+            return raw
+
+        raw_x = {}
+        raw_w = {}
+        for c in (0, 1):
+            raw_x[c] = load(x_rows[c])
+        for w in (0, 1):
+            raw_w[w] = load(w_rows[0, w])
+        for c in (2, 3):
+            raw_x[c] = load(x_rows[c])
+        for w in range(2, W_PIECES):
+            raw_w[w] = load(w_rows[w // 2, w % 2])
+
+        ident = const.tile([P, P], F32)
+        make_identity(nc, ident[:])
+        warm_in = const.tile([P, 1], F32)
+        warm_out = const.tile([P, 1], F32)
+        nc.vector.memset(warm_in[:], 0.0)
+        nc.scalar.activation(out=warm_out[:], in_=warm_in[:], func=ACT.Sigmoid)
+
+        x_codes = const.tile([P, BATCH], U32, align_bytes=64)
+        x_scales = const.tile([P, BATCH], U8, align_bytes=64)
+
+        def transpose_words(raw):
+            bank = psum.tile([P, BANK], F32, tag="work", bufs=5)
+            words = raw[:].bitcast(F32)
+            for s in range(BANK // P):
+                cols = slice(s * P, (s + 1) * P)
+                nc.tensor.transpose(out=bank[:, cols], in_=words[:, cols], identity=ident[:])
+            return bank
+
+        def regroup(copy, bank):
+            grouped = grouped_pool.tile([P, PIECE * PACK], BF16, tag="grouped", align_bytes=64)
+            copy(
+                out=grouped[:].bitcast(F32).rearrange("p (a r u) -> p a r u", a=2, u=2),
+                in_=bank[:].rearrange("p (a u r) -> p a r u", a=2, u=2),
+            )
+            return grouped
+
+        def quantise(grouped, codes, scales):
+            nc.vector.quantize_mx(out=codes.bitcast(FP8X4), scales=scales, in_=grouped[:])
+
+        def quantise_x(c, grouped):
+            cols = slice(c * PIECE, (c + 1) * PIECE)
+            quantise(grouped, x_codes[:, cols], x_scales[:, cols])
+
+        w_mx = {}
+
+        def quantise_w(w, grouped):
+            w_codes = w_mx_pool.tile([P, PIECE], U32, tag="w_codes", align_bytes=64)
+            w_scales = w_mx_pool.tile([P, PIECE], U8, tag="w_scales", align_bytes=64)
+            quantise(grouped, w_codes[:], w_scales[:])
+            w_mx[w] = (w_codes, w_scales)
+
+        gate_bank = {}
+        cell = {}
+
+        def multiply(unit, e):
+            j, n = divmod(unit, HALVES)
+            w_codes, w_scales = w_mx[2 * j + e]
+            batch = slice(n * BANK, (n + 1) * BANK)
+            for h in range(2):
+                hidden = slice(h * P, (h + 1) * P)
+                bank = psum.tile([P, BANK], F32, tag="work", bufs=5)
+                nc.tensor.matmul_mx(
+                    out=bank[:],
+                    lhsT=w_codes[:, hidden].bitcast(FP8X4),
+                    lhsT_scale=w_scales[:, hidden],
+                    rhs=x_codes[:, batch].bitcast(FP8X4),
+                    rhs_scale=x_scales[:, batch],
+                    start=True,
+                    stop=True,
+                )
+                gate_bank[unit, 2 * h + e] = bank
+
+        def activate_gate(unit, gate, func, name):
+            j = unit // HALVES
+            col = gate * HID_BLOCKS + j
+            act = cell_pool.tile([P, BANK], F32, tag=name)
+            nc.scalar.activation(
+                out=act[:], in_=gate_bank[unit, gate][:], func=func, bias=bias[:, col : col + 1]
+            )
+            cell[unit, name] = act
+
+        def input_times_candidate(unit):
+            ig = cell_pool.tile([P, BANK], F32, tag="ig")
+            nc.vector.tensor_tensor(
+                out=ig[:], in0=cell[unit, "i"][:], in1=cell[unit, "g"][:], op=ALU.mult
+            )
+            cell[unit, "ig"] = ig
+
+        def new_cell_state(unit):
+            j = unit // HALVES
+            c_new = cell_pool.tile([P, BANK], F32, tag="c_new")
+            nc.vector.scalar_tensor_tensor(
+                out=c_new[:],
+                in0=cell[unit, "f"][:],
+                scalar=c_start[:, j : j + 1],
+                in1=cell[unit, "ig"][:],
+                op0=ALU.mult,
+                op1=ALU.add,
+            )
+            cell[unit, "c_new"] = c_new
+
+        def batch_onto_partitions(unit, name, tag, bufs):
+            bank = psum.tile([P, BANK], F32, tag=tag, bufs=bufs)
+            for t in range(BANK // P):
+                cols = slice(t * P, (t + 1) * P)
+                nc.tensor.transpose(
+                    out=bank[:, cols], in_=cell[unit, name][:, cols], identity=ident[:]
+                )
+            cell[unit, tag] = bank
+
+        def tanh_of_cell_state(unit):
+            tanh_c = cell_pool.tile([P, BANK], F32, tag="tanh_c")
+            nc.scalar.activation(out=tanh_c[:], in_=cell[unit, "c_T"][:], func=ACT.Tanh)
+            cell[unit, "tanh_c"] = tanh_c
+
+        out_blocks = out.rearrange("(n t p) (j c) -> n j p t c", t=BANK // P, p=P, c=P)
+
+        def hidden_state(unit):
+            j, n = divmod(unit, HALVES)
+            h_new = cell_pool.tile([P, BANK], F32, tag="h_new")
+            nc.vector.tensor_tensor(
+                out=h_new[:], in0=cell[unit, "o_T"][:], in1=cell[unit, "tanh_c"][:], op=ALU.mult
+            )
+            nc.sync.dma_start(
+                out=out_blocks[n, j], in_=h_new[:].rearrange("p (t c) -> p t c", c=P)
+            )
+
+        grouped_x = {}
+        grouped_w = {}
+        for c in (0, 1):
+            grouped_x[c] = regroup(nc.scalar.copy, transpose_words(raw_x[c]))
+
+        vector_rows_f32 = const.tile([P, P], F32)
+        nc.vector.tensor_copy(out=vector_rows_f32[:], in_=vector_rows[:])
+        vector_bank = psum.tile([P, BANK], F32, tag="work", bufs=5)
+        nc.tensor.transpose(out=vector_bank[:, 0:P], in_=vector_rows_f32[:], identity=ident[:])
+        vector_cols = const.tile([P, P], F32)
+        nc.vector.tensor_copy(out=vector_cols[:], in_=vector_bank[:, 0:P])
+        c_start = vector_cols[:, 3 * VECTOR_ROWS : 3 * VECTOR_ROWS + HID_BLOCKS]
+
+        for c in (0, 1):
+            quantise_x(c, grouped_x[c])
+        grouped_w[0] = regroup(nc.scalar.copy, transpose_words(raw_w[0]))
+
+        bias_ih_hh = const.tile([P, VECTOR_ROWS], F32)
+        bias = const.tile([P, VECTOR_ROWS], F32)
+        nc.vector.tensor_tensor(
+            out=bias_ih_hh[:],
+            in0=vector_cols[:, VECTOR_ROWS : 2 * VECTOR_ROWS],
+            in1=vector_cols[:, 2 * VECTOR_ROWS : 3 * VECTOR_ROWS],
+            op=ALU.add,
+        )
+        nc.vector.tensor_tensor(
+            out=bias[:], in0=vector_cols[:, 0:VECTOR_ROWS], in1=bias_ih_hh[:], op=ALU.add
+        )
+
+        quantise_w(0, grouped_w[0])
+        grouped_w[1] = regroup(nc.vector.tensor_copy, transpose_words(raw_w[1]))
+        grouped_x[2] = regroup(nc.vector.tensor_copy, transpose_words(raw_x[2]))
+        multiply(0, 0)
+        quantise_w(1, grouped_w[1])
+        grouped_x[3] = regroup(nc.vector.tensor_copy, transpose_words(raw_x[3]))
+        multiply(0, 1)
+        quantise_x(2, grouped_x[2])
+        quantise_x(3, grouped_x[3])
+        grouped_w[2] = regroup(nc.vector.tensor_copy, transpose_words(raw_w[2]))
+
+        w_bank = {}
+        for t in range(UNITS + 1):
+            if t + 3 < W_PIECES:
+                w_bank[t + 3] = transpose_words(raw_w[t + 3])
+            if t < UNITS:
+                activate_gate(t, GATE_I, ACT.Sigmoid, "i")
+                activate_gate(t, GATE_G, ACT.Tanh, "g")
+                activate_gate(t, GATE_F, ACT.Sigmoid, "f")
+                activate_gate(t, GATE_O, ACT.Sigmoid, "o")
+            if t >= 1:
+                tanh_of_cell_state(t - 1)
+            if t < UNITS:
+                input_times_candidate(t)
+            if t + 2 < W_PIECES:
+                quantise_w(t + 2, grouped_w[t + 2])
+            if t + 1 < UNITS:
+                multiply(t + 1, 0)
+                multiply(t + 1, 1)
+            if t < UNITS:
+                new_cell_state(t)
+                batch_onto_partitions(t, "c_new", "c_T", 1)
+                batch_onto_partitions(t, "o", "o_T", 2)
+            if t >= 1:
+                hidden_state(t - 1)
+            if t + 3 < W_PIECES:
+                grouped_w[t + 3] = regroup(nc.vector.tensor_copy, w_bank[t + 3])

@@ -23,6 +23,7 @@ HALVES = BATCH // BANK
 UNITS = HID_BLOCKS * HALVES
 GATE_I, GATE_F, GATE_G, GATE_O = 0, 1, 2, 3
 VECTOR_ROWS = GATES * HID // P
+LAST_UNIT_PARTS = 2
 
 FLOPS = 2 * BATCH * GATES * HID * K
 
@@ -142,38 +143,51 @@ def tile_rdecommunicationlstm_pa_kernel(
             )
             cell[unit, name] = act
 
+        def parts_of(unit):
+            parts = LAST_UNIT_PARTS if unit == UNITS - 1 else 1
+            width = BANK // parts
+            return [(k * width, (k + 1) * width) for k in range(parts)]
+
         def input_times_candidate(unit):
             ig = cell_pool.tile([P, BANK], F32, tag="ig")
-            nc.vector.tensor_tensor(
-                out=ig[:], in0=cell[unit, "i"][:], in1=cell[unit, "g"][:], op=ALU.mult
-            )
+            for lo, hi in parts_of(unit):
+                nc.vector.tensor_tensor(
+                    out=ig[:, lo:hi],
+                    in0=cell[unit, "i"][:, lo:hi],
+                    in1=cell[unit, "g"][:, lo:hi],
+                    op=ALU.mult,
+                )
             cell[unit, "ig"] = ig
 
         def new_cell_state(unit):
             j = unit // HALVES
             c_new = cell_pool.tile([P, BANK], F32, tag="c_new")
-            nc.vector.scalar_tensor_tensor(
-                out=c_new[:],
-                in0=cell[unit, "f"][:],
-                scalar=c_start[:, j : j + 1],
-                in1=cell[unit, "ig"][:],
-                op0=ALU.mult,
-                op1=ALU.add,
-            )
+            for lo, hi in parts_of(unit):
+                nc.vector.scalar_tensor_tensor(
+                    out=c_new[:, lo:hi],
+                    in0=cell[unit, "f"][:, lo:hi],
+                    scalar=c_start[:, j : j + 1],
+                    in1=cell[unit, "ig"][:, lo:hi],
+                    op0=ALU.mult,
+                    op1=ALU.add,
+                )
             cell[unit, "c_new"] = c_new
 
-        def batch_onto_partitions(unit, name, tag, bufs):
-            bank = psum.tile([P, BANK], F32, tag=tag, bufs=bufs)
-            for t in range(BANK // P):
-                cols = slice(t * P, (t + 1) * P)
+        def batch_onto_partitions(unit, name, lo, hi):
+            bank = psum.tile([P, BANK], F32, tag="back", bufs=3)
+            for first in range(lo, hi, P):
+                block = slice(first, first + P)
                 nc.tensor.transpose(
-                    out=bank[:, cols], in_=cell[unit, name][:, cols], identity=ident[:]
+                    out=bank[:, block], in_=cell[unit, name][:, block], identity=ident[:]
                 )
-            cell[unit, tag] = bank
+            return bank
 
         def tanh_of_cell_state(unit):
             tanh_c = cell_pool.tile([P, BANK], F32, tag="tanh_c")
-            nc.scalar.activation(out=tanh_c[:], in_=cell[unit, "c_T"][:], func=ACT.Tanh)
+            for lo, hi in parts_of(unit):
+                nc.scalar.activation(
+                    out=tanh_c[:, lo:hi], in_=cell[unit, "c_T", lo][:, lo:hi], func=ACT.Tanh
+                )
             cell[unit, "tanh_c"] = tanh_c
 
         out_blocks = out.rearrange("(n t p) (j c) -> n j p t c", t=BANK // P, p=P, c=P)
@@ -181,12 +195,17 @@ def tile_rdecommunicationlstm_pa_kernel(
         def hidden_state(unit):
             j, n = divmod(unit, HALVES)
             h_new = cell_pool.tile([P, BANK], F32, tag="h_new")
-            nc.vector.tensor_tensor(
-                out=h_new[:], in0=cell[unit, "o_T"][:], in1=cell[unit, "tanh_c"][:], op=ALU.mult
-            )
-            nc.sync.dma_start(
-                out=out_blocks[n, j], in_=h_new[:].rearrange("p (t c) -> p t c", c=P)
-            )
+            for lo, hi in parts_of(unit):
+                nc.vector.tensor_tensor(
+                    out=h_new[:, lo:hi],
+                    in0=cell[unit, "o_T"][:, lo:hi],
+                    in1=cell[unit, "tanh_c"][:, lo:hi],
+                    op=ALU.mult,
+                )
+                nc.sync.dma_start(
+                    out=out_blocks[n, j, :, lo // P : hi // P, :],
+                    in_=h_new[:, lo:hi].rearrange("p (t c) -> p t c", c=P),
+                )
 
         grouped_x = {}
         grouped_w = {}
@@ -203,7 +222,13 @@ def tile_rdecommunicationlstm_pa_kernel(
 
         for c in (0, 1):
             quantise_x(c, grouped_x[c])
-        grouped_w[0] = regroup(nc.scalar.copy, transpose_words(raw_w[0]))
+        for w in (0, 1):
+            grouped_w[w] = regroup(nc.scalar.copy, transpose_words(raw_w[w]))
+        x_bank = {}
+        for c in (2, 3):
+            x_bank[c] = transpose_words(raw_x[c])
+        quantise_w(0, grouped_w[0])
+        multiply(0, 0)
 
         bias_ih_hh = const.tile([P, VECTOR_ROWS], F32)
         bias = const.tile([P, VECTOR_ROWS], F32)
@@ -213,22 +238,18 @@ def tile_rdecommunicationlstm_pa_kernel(
             in1=vector_cols[:, 2 * VECTOR_ROWS : 3 * VECTOR_ROWS],
             op=ALU.add,
         )
+        grouped_x[2] = regroup(nc.vector.tensor_copy, x_bank[2])
         nc.vector.tensor_tensor(
             out=bias[:], in0=vector_cols[:, 0:VECTOR_ROWS], in1=bias_ih_hh[:], op=ALU.add
         )
-
-        quantise_w(0, grouped_w[0])
-        grouped_w[1] = regroup(nc.vector.tensor_copy, transpose_words(raw_w[1]))
-        grouped_x[2] = regroup(nc.vector.tensor_copy, transpose_words(raw_x[2]))
-        multiply(0, 0)
         quantise_w(1, grouped_w[1])
-        grouped_x[3] = regroup(nc.vector.tensor_copy, transpose_words(raw_x[3]))
         multiply(0, 1)
+        grouped_x[3] = regroup(nc.vector.tensor_copy, x_bank[3])
         quantise_x(2, grouped_x[2])
+        w_bank = {2: transpose_words(raw_w[2])}
         quantise_x(3, grouped_x[3])
-        grouped_w[2] = regroup(nc.vector.tensor_copy, transpose_words(raw_w[2]))
+        grouped_w[2] = regroup(nc.vector.tensor_copy, w_bank[2])
 
-        w_bank = {}
         for t in range(UNITS + 1):
             if t + 3 < W_PIECES:
                 w_bank[t + 3] = transpose_words(raw_w[t + 3])
@@ -248,9 +269,10 @@ def tile_rdecommunicationlstm_pa_kernel(
                 multiply(t + 1, 1)
             if t < UNITS:
                 new_cell_state(t)
-                batch_onto_partitions(t, "c_new", "c_T", 1)
-                batch_onto_partitions(t, "o", "o_T", 2)
-            if t >= 1:
-                hidden_state(t - 1)
+                for lo, hi in parts_of(t):
+                    cell[t, "c_T", lo] = batch_onto_partitions(t, "c_new", lo, hi)
+                cell[t, "o_T"] = batch_onto_partitions(t, "o", 0, BANK)
             if t + 3 < W_PIECES:
                 grouped_w[t + 3] = regroup(nc.vector.tensor_copy, w_bank[t + 3])
+            if t >= 1:
+                hidden_state(t - 1)

@@ -224,9 +224,8 @@ def tile_rdecommunicationlstm_pa_kernel(
             quantise_x(c, grouped_x[c])
         for w in (0, 1):
             grouped_w[w] = regroup(nc.scalar.copy, transpose_words(raw_w[w]))
-        x_bank = {}
         for c in (2, 3):
-            x_bank[c] = transpose_words(raw_x[c])
+            grouped_x[c] = regroup(nc.scalar.copy, transpose_words(raw_x[c]))
         quantise_w(0, grouped_w[0])
         multiply(0, 0)
 
@@ -238,16 +237,14 @@ def tile_rdecommunicationlstm_pa_kernel(
             in1=vector_cols[:, 2 * VECTOR_ROWS : 3 * VECTOR_ROWS],
             op=ALU.add,
         )
-        grouped_x[2] = regroup(nc.vector.tensor_copy, x_bank[2])
+        quantise_w(1, grouped_w[1])
         nc.vector.tensor_tensor(
             out=bias[:], in0=vector_cols[:, 0:VECTOR_ROWS], in1=bias_ih_hh[:], op=ALU.add
         )
-        quantise_w(1, grouped_w[1])
-        multiply(0, 1)
-        grouped_x[3] = regroup(nc.vector.tensor_copy, x_bank[3])
-        quantise_x(2, grouped_x[2])
         w_bank = {2: transpose_words(raw_w[2])}
-        quantise_x(3, grouped_x[3])
+        multiply(0, 1)
+        for c in (2, 3):
+            quantise_x(c, grouped_x[c])
         grouped_w[2] = regroup(nc.vector.tensor_copy, w_bank[2])
 
         for t in range(UNITS + 1):

from contextlib import ExitStack

import concourse.mybir as mybir
from concourse.masks import make_identity

F32 = mybir.dt.float32
BF16 = mybir.dt.bfloat16
U32 = mybir.dt.uint32
U8 = mybir.dt.uint8
FP8X4 = mybir.dt.float8_e4m3fn_x4
ACT = mybir.ActivationFunctionType
ALU = mybir.AluOpType

P = 128
BATCH, K, HID, GATES = 1024, 512, 1024, 4
PACK = 4
BANK = 512
PIECE = 2 * P
X_PIECES = BATCH // PIECE
W_PIECES = GATES * HID // PIECE
HID_BLOCKS = HID // P
HALVES = BATCH // BANK
UNITS = HID_BLOCKS * HALVES
GATE_I, GATE_F, GATE_G, GATE_O = 0, 1, 2, 3
VECTOR_ROWS = GATES * HID // P
LAST_UNIT_PARTS = 2

FLOPS = 2 * BATCH * GATES * HID * K


def tile_rdecommunicationlstm_pa_kernel(
    tc, regime_vector, W_ih0, hh_gates, b_ih0, b_hh0, c_init, out
):
    nc = tc.nc
    with ExitStack() as ctx:
        const = ctx.enter_context(tc.tile_pool(name="const", bufs=1))
        raw_pool = ctx.enter_context(tc.tile_pool(name="raw", bufs=X_PIECES + W_PIECES))
        grouped_pool = ctx.enter_context(tc.tile_pool(name="grouped", bufs=4))
        w_mx_pool = ctx.enter_context(tc.tile_pool(name="w_mx", bufs=W_PIECES))
        cell_pool = ctx.enter_context(tc.tile_pool(name="cell", bufs=3))
        psum = ctx.enter_context(tc.psum_pool(name="psum", bufs=1))
        ctx.enter_context(tc.manual_schedule())

        vector_rows = const.tile([P, P], BF16)
        nc.vector.memset(vector_rows[:], 0.0)
        for slot, vec in enumerate((hh_gates, b_ih0, b_hh0)):
            nc.scalar.dma_start(
                out=vector_rows[slot * VECTOR_ROWS : (slot + 1) * VECTOR_ROWS, :],
                in_=vec.rearrange("(r c) -> r c", c=P),
            )
        nc.scalar.dma_start(
            out=vector_rows[3 * VECTOR_ROWS : 3 * VECTOR_ROWS + HID_BLOCKS, :],
            in_=c_init.rearrange("(r c) -> r c", c=P),
        )

        x_rows = regime_vector.rearrange("(c a p) k -> c p a k", a=2, p=P)
        w_rows = W_ih0.rearrange("(h e j p) k -> j e p h k", h=2, e=2, p=P)

        def load(rows):
            raw = raw_pool.tile([P, 2 * K], BF16, tag="raw")
            nc.sync.dma_start(out=raw[:].rearrange("p (a k) -> p a k", a=2), in_=rows)
            return raw

        raw_x = {}
        raw_w = {}
        for c in (0, 1):
            raw_x[c] = load(x_rows[c])
        for w in (0, 1):
            raw_w[w] = load(w_rows[0, w])
        for c in (2, 3):
            raw_x[c] = load(x_rows[c])
        for w in range(2, W_PIECES):
            raw_w[w] = load(w_rows[w // 2, w % 2])

        ident = const.tile([P, P], F32)
        make_identity(nc, ident[:])
        warm_in = const.tile([P, 1], F32)
        warm_out = const.tile([P, 1], F32)
        nc.vector.memset(warm_in[:], 0.0)
        nc.scalar.activation(out=warm_out[:], in_=warm_in[:], func=ACT.Sigmoid)

        x_codes = const.tile([P, BATCH], U32, align_bytes=64)
        x_scales = const.tile([P, BATCH], U8, align_bytes=64)

        def transpose_words(raw):
            bank = psum.tile([P, BANK], F32, tag="work", bufs=5)
            words = raw[:].bitcast(F32)
            for s in range(BANK // P):
                cols = slice(s * P, (s + 1) * P)
                nc.tensor.transpose(out=bank[:, cols], in_=words[:, cols], identity=ident[:])
            return bank

        def regroup(copy, bank):
            grouped = grouped_pool.tile([P, PIECE * PACK], BF16, tag="grouped", align_bytes=64)
            copy(
                out=grouped[:].bitcast(F32).rearrange("p (a r u) -> p a r u", a=2, u=2),
                in_=bank[:].rearrange("p (a u r) -> p a r u", a=2, u=2),
            )
            return grouped

        def quantise(grouped, codes, scales):
            nc.vector.quantize_mx(out=codes.bitcast(FP8X4), scales=scales, in_=grouped[:])

        def quantise_x(c, grouped):
            cols = slice(c * PIECE, (c + 1) * PIECE)
            quantise(grouped, x_codes[:, cols], x_scales[:, cols])

        w_mx = {}

        def quantise_w(w, grouped):
            w_codes = w_mx_pool.tile([P, PIECE], U32, tag="w_codes", align_bytes=64)
            w_scales = w_mx_pool.tile([P, PIECE], U8, tag="w_scales", align_bytes=64)
            quantise(grouped, w_codes[:], w_scales[:])
            w_mx[w] = (w_codes, w_scales)

        gate_bank = {}
        cell = {}

        def multiply(unit, e):
            j, n = divmod(unit, HALVES)
            w_codes, w_scales = w_mx[2 * j + e]
            batch = slice(n * BANK, (n + 1) * BANK)
            for h in range(2):
                hidden = slice(h * P, (h + 1) * P)
                bank = psum.tile([P, BANK], F32, tag="work", bufs=5)
                nc.tensor.matmul_mx(
                    out=bank[:],
                    lhsT=w_codes[:, hidden].bitcast(FP8X4),
                    lhsT_scale=w_scales[:, hidden],
                    rhs=x_codes[:, batch].bitcast(FP8X4),
                    rhs_scale=x_scales[:, batch],
                    start=True,
                    stop=True,
                )
                gate_bank[unit, 2 * h + e] = bank

        def activate_gate(unit, gate, func, name):
            j = unit // HALVES
            col = gate * HID_BLOCKS + j
            act = cell_pool.tile([P, BANK], F32, tag=name)
            nc.scalar.activation(
                out=act[:], in_=gate_bank[unit, gate][:], func=func, bias=bias[:, col : col + 1]
            )
            cell[unit, name] = act

        def parts_of(unit):
            parts = LAST_UNIT_PARTS if unit == UNITS - 1 else 1
            width = BANK // parts
            return [(k * width, (k + 1) * width) for k in range(parts)]

        def input_times_candidate(unit):
            ig = cell_pool.tile([P, BANK], F32, tag="ig")
            for lo, hi in parts_of(unit):
                nc.vector.tensor_tensor(
                    out=ig[:, lo:hi],
                    in0=cell[unit, "i"][:, lo:hi],
                    in1=cell[unit, "g"][:, lo:hi],
                    op=ALU.mult,
                )
            cell[unit, "ig"] = ig

        def new_cell_state(unit):
            j = unit // HALVES
            c_new = cell_pool.tile([P, BANK], F32, tag="c_new")
            for lo, hi in parts_of(unit):
                nc.vector.scalar_tensor_tensor(
                    out=c_new[:, lo:hi],
                    in0=cell[unit, "f"][:, lo:hi],
                    scalar=c_start[:, j : j + 1],
                    in1=cell[unit, "ig"][:, lo:hi],
                    op0=ALU.mult,
                    op1=ALU.add,
                )
            cell[unit, "c_new"] = c_new

        def batch_onto_partitions(unit, name, lo, hi):
            bank = psum.tile([P, BANK], F32, tag="back", bufs=3)
            for first in range(lo, hi, P):
                block = slice(first, first + P)
                nc.tensor.transpose(
                    out=bank[:, block], in_=cell[unit, name][:, block], identity=ident[:]
                )
            return bank

        def tanh_of_cell_state(unit):
            tanh_c = cell_pool.tile([P, BANK], F32, tag="tanh_c")
            for lo, hi in parts_of(unit):
                nc.scalar.activation(
                    out=tanh_c[:, lo:hi], in_=cell[unit, "c_T", lo][:, lo:hi], func=ACT.Tanh
                )
            cell[unit, "tanh_c"] = tanh_c

        out_blocks = out.rearrange("(n t p) (j c) -> n j p t c", t=BANK // P, p=P, c=P)

        def hidden_state(unit):
            j, n = divmod(unit, HALVES)
            h_new = cell_pool.tile([P, BANK], F32, tag="h_new")
            for lo, hi in parts_of(unit):
                nc.vector.tensor_tensor(
                    out=h_new[:, lo:hi],
                    in0=cell[unit, "o_T"][:, lo:hi],
                    in1=cell[unit, "tanh_c"][:, lo:hi],
                    op=ALU.mult,
                )
                nc.sync.dma_start(
                    out=out_blocks[n, j, :, lo // P : hi // P, :],
                    in_=h_new[:, lo:hi].rearrange("p (t c) -> p t c", c=P),
                )

        grouped_x = {}
        grouped_w = {}
        for c in (0, 1):
            grouped_x[c] = regroup(nc.scalar.copy, transpose_words(raw_x[c]))

        vector_rows_f32 = const.tile([P, P], F32)
        nc.vector.tensor_copy(out=vector_rows_f32[:], in_=vector_rows[:])
        vector_bank = psum.tile([P, BANK], F32, tag="work", bufs=5)
        nc.tensor.transpose(out=vector_bank[:, 0:P], in_=vector_rows_f32[:], identity=ident[:])
        vector_cols = const.tile([P, P], F32)
        nc.vector.tensor_copy(out=vector_cols[:], in_=vector_bank[:, 0:P])
        c_start = vector_cols[:, 3 * VECTOR_ROWS : 3 * VECTOR_ROWS + HID_BLOCKS]

        for c in (0, 1):
            quantise_x(c, grouped_x[c])
        for w in (0, 1):
            grouped_w[w] = regroup(nc.scalar.copy, transpose_words(raw_w[w]))
        for c in (2, 3):
            grouped_x[c] = regroup(nc.scalar.copy, transpose_words(raw_x[c]))
        quantise_w(0, grouped_w[0])
        multiply(0, 0)

        bias_ih_hh = const.tile([P, VECTOR_ROWS], F32)
        bias = const.tile([P, VECTOR_ROWS], F32)
        nc.vector.tensor_tensor(
            out=bias_ih_hh[:],
            in0=vector_cols[:, VECTOR_ROWS : 2 * VECTOR_ROWS],
            in1=vector_cols[:, 2 * VECTOR_ROWS : 3 * VECTOR_ROWS],
            op=ALU.add,
        )
        quantise_w(1, grouped_w[1])
        nc.vector.tensor_tensor(
            out=bias[:], in0=vector_cols[:, 0:VECTOR_ROWS], in1=bias_ih_hh[:], op=ALU.add
        )
        w_bank = {2: transpose_words(raw_w[2])}
        multiply(0, 1)
        for c in (2, 3):
            quantise_x(c, grouped_x[c])
        grouped_w[2] = regroup(nc.vector.tensor_copy, w_bank[2])

        for t in range(UNITS + 1):
            if t + 3 < W_PIECES:
                w_bank[t + 3] = transpose_words(raw_w[t + 3])
            if t < UNITS:
                activate_gate(t, GATE_I, ACT.Sigmoid, "i")
                activate_gate(t, GATE_G, ACT.Tanh, "g")
                activate_gate(t, GATE_F, ACT.Sigmoid, "f")
                activate_gate(t, GATE_O, ACT.Sigmoid, "o")
            if t >= 1:
                tanh_of_cell_state(t - 1)
            if t < UNITS:
                input_times_candidate(t)
            if t + 2 < W_PIECES:
                quantise_w(t + 2, grouped_w[t + 2])
            if t + 1 < UNITS:
                multiply(t + 1, 0)
                multiply(t + 1, 1)
            if t < UNITS:
                new_cell_state(t)
                for lo, hi in parts_of(t):
                    cell[t, "c_T", lo] = batch_onto_partitions(t, "c_new", lo, hi)
                cell[t, "o_T"] = batch_onto_partitions(t, "o", 0, BANK)
            if t + 3 < W_PIECES:
                grouped_w[t + 3] = regroup(nc.vector.tensor_copy, w_bank[t + 3])
            if t >= 1:
                hidden_state(t - 1)
